import numpy as np
import ml_dtypes


def mxq(x, axis, fmt="e4m3"):
    dtype, down = {"e4m3": (ml_dtypes.float8_e4m3fn, 7), "e5m2": (ml_dtypes.float8_e5m2, 14)}[fmt]
    v = np.moveaxis(np.asarray(x, np.float32).astype(ml_dtypes.bfloat16).astype(np.float64), axis, -1)
    blocks = v.reshape(v.shape[:-1] + (-1, 32))
    amax = np.abs(blocks).max(-1, keepdims=True)
    byte = np.maximum(np.where(amax > 0, np.frexp(amax)[1] - 1 + 127, 0) - down, 1)
    scale = np.exp2(byte - 127.0)
    codes = (blocks / scale).astype(np.float32).astype(dtype).astype(np.float64)
    return np.moveaxis((codes * scale).reshape(v.shape), -1, axis)


WIDE = False


def mx_kscale(k):
    if not WIDE:
        return np.ones(k)
    levels = np.array([10, -10, 5, -5, 0])
    a = np.random.permutation(np.resize(levels, k // 512 * 4)).reshape(k // 512, 4)
    idx = np.arange(k)
    return np.exp2(a[idx // 512, idx % 128 // 32])


BF16 = ml_dtypes.bfloat16


def bf(x):
    return np.asarray(x, np.float32).astype(BF16)


def f64(x):
    return np.asarray(x).astype(np.float64)


E2M1 = np.array([0.0, 0.5, 1.0, 1.5, 2.0, 3.0, 4.0, 6.0, -0.0, -0.5, -1.0, -1.5, -2.0, -3.0, -4.0, -6.0])


def pack_weight(w, fmt):
    k, n = w.shape
    w = f64(bf(w)).reshape(k // 32, 32, n)
    amax = np.abs(w).max(1)
    if fmt == "e4m3":
        byte = np.frexp(amax)[1] - 1 + 127 - 7
    else:
        mant, ex = np.frexp(amax / 6.0)
        byte = np.where(mant > 0.5, ex, ex - 1) + 127
    byte = np.clip(np.where(amax > 0, byte, 1), 1, 254)
    scaled = (w * np.exp2(127.0 - byte)[:, None, :]).reshape(k, n).astype(np.float32)
    by_word = np.ascontiguousarray(scaled.reshape(k // 512, 128, 4, n).transpose(0, 1, 3, 2))
    if fmt == "e4m3":
        words = by_word.astype(ml_dtypes.float8_e4m3fn).view(np.uint8)
    else:
        c = by_word.astype(ml_dtypes.float4_e2m1fn).view(np.uint8) & 0xF
        words = c[..., 0::2] | (c[..., 1::2] << 4)
    return np.ascontiguousarray(words), np.ascontiguousarray(byte.astype(np.uint8).reshape(k // 512, 16, n))


def unpack_weight(words, scales, fmt):
    g, p, n, _ = words.shape
    if fmt == "e4m3":
        vals = np.ascontiguousarray(words).view(ml_dtypes.float8_e4m3fn).astype(np.float64)
    else:
        nib = np.empty((g, p, n, 4), np.uint8)
        nib[..., 0::2] = words & 0xF
        nib[..., 1::2] = words >> 4
        vals = E2M1[nib]
    vals = vals * np.repeat(np.exp2(scales.astype(np.float64) - 127.0), 8, axis=1)[..., None]
    return vals.transpose(0, 1, 3, 2).reshape(g * 512, n)


N, T, D, B0, C, P0, V1, P1, V2 = 2, 256, 16384, 2046, 2, 512, 2048, 512, 1024
SIG = 2.0
FMT = "e4m3"


def softmax(v):
    e = np.exp(v - v.max(-1, keepdims=True))
    return e / e.sum(-1, keepdims=True)


def setup_inputs():
    s, t = mx_kscale(D), mx_kscale(P1)
    x = bf(np.random.standard_normal((N, T, D)) * s)
    tail_proj_1_words, tail_proj_1_scales = pack_weight(np.random.standard_normal((D, P1)) / np.sqrt(D) / s[:, None] * t, FMT)
    tail_w_1_words, tail_w_1_scales = pack_weight(np.random.standard_normal((P1, V2)) * SIG / np.sqrt(P1) / t[:, None], FMT)
    cluster_prob = bf(1.0 / (1.0 + np.exp(0.7 - 1.5 * np.random.standard_normal((N, T, 1)))))
    return {"x": x,
            "tail_proj_1_words": tail_proj_1_words,
            "tail_proj_1_scales": tail_proj_1_scales,
            "tail_w_1_words": tail_w_1_words,
            "tail_w_1_scales": tail_w_1_scales,
            "cluster_prob": cluster_prob}


def reference(x, tail_proj_1_words, tail_proj_1_scales, tail_w_1_words, tail_w_1_scales, cluster_prob):
    h = mxq(f64(x), 2, "e4m3") @ unpack_weight(tail_proj_1_words, tail_proj_1_scales, FMT)
    tail_sm = softmax(mxq(h, 2, "e4m3") @ unpack_weight(tail_w_1_words, tail_w_1_scales, FMT))
    return tail_sm * f64(cluster_prob)

@@ -1,0 +1,319 @@
+from contextlib import ExitStack
+
+import concourse.mybir as mybir
+from concourse.masks import make_identity
+
+F32 = mybir.dt.float32
+BF16 = mybir.dt.bfloat16
+I32 = mybir.dt.int32
+U32 = mybir.dt.uint32
+U8 = mybir.dt.uint8
+FP8X4 = mybir.dt.float8_e4m3fn_x4
+EXP = mybir.ActivationFunctionType.Exp
+ALU = mybir.AluOpType
+
+P = 128
+PACK = 4
+K_PASS = P * PACK
+PAIRS = PACK // 2
+TOKENS = 512
+D = 16384
+P1 = 512
+V2 = 1024
+BANK = 512
+PSUM_BANKS = 8
+
+TOKEN_TILES = TOKENS // P
+PASSES = D // K_PASS
+ROUND_PASSES = 8
+ROUND_K = ROUND_PASSES * K_PASS
+CHUNKS = PASSES // ROUND_PASSES
+ROUNDS = CHUNKS * TOKEN_TILES
+LAST_CHUNK = ROUNDS - TOKEN_TILES
+BANK_PASSES = BANK // (PAIRS * P)
+PIECE_PASSES = 2
+PIECES = PASSES // PIECE_PASSES
+PIECES_AHEAD = 2
+X_BUFS = 8
+PLANE_STEP = 4
+SHARED_PLANES = 4
+PLANE_SLOTS = PASSES // SHARED_PLANES
+QUADRANT = 32
+HALVES = V2 // BANK
+
+FLOPS = 2 * TOKENS * D * P1 + 2 * TOKENS * P1 * V2
+
+
+def tile_adaptiveinputsoftmax_pb_k_kernel(
+    tc,
+    x,
+    tail_proj_1_words,
+    tail_proj_1_scales,
+    tail_w_1_words,
+    tail_w_1_scales,
+    cluster_prob,
+    out,
+):
+    nc = tc.nc
+    x_rows = x.flatten_outer_dims()
+    out_rows = out.flatten_outer_dims()
+    w1_words_dram = tail_proj_1_words.rearrange("g p n t -> p g (n t)").bitcast(I32)
+    w2_words_dram = tail_w_1_words.rearrange("o p n t -> (o p) (n t)").bitcast(I32)
+    w1_scales_dram = tail_proj_1_scales.bitcast(I32).rearrange("(s j) q n -> q j s n", j=SHARED_PLANES)
+    w2_scales_dram = tail_w_1_scales.bitcast(I32).rearrange("o (c r) n -> (o r) c n", r=PLANE_STEP)
+
+    with ExitStack() as ctx:
+        ctx.enter_context(tc.manual_schedule())
+        const = ctx.enter_context(tc.tile_pool(name="const", bufs=1))
+        weights = ctx.enter_context(tc.tile_pool(name="weights", bufs=1))
+        raw_pool = ctx.enter_context(tc.tile_pool(name="raw", bufs=X_BUFS))
+        work = ctx.enter_context(tc.tile_pool(name="work", bufs=2))
+        probs_pool = ctx.enter_context(tc.tile_pool(name="probs", bufs=3))
+        stats = ctx.enter_context(tc.tile_pool(name="stats", bufs=4))
+        psum = ctx.enter_context(tc.psum_pool(name="psum", bufs=PSUM_BANKS))
+
+        x_raw = {}
+        x_sorted = {}
+        x_grouped = {}
+        x_codes = {}
+        x_scales = {}
+        w1_words = {}
+        h_acc = {}
+        h_bf16 = {}
+        h_codes = {}
+        h_scales = {}
+        logits = {}
+        neg_max = {}
+        probs = {}
+        half_sum = {}
+
+        def load_x(r):
+            chunk, i = divmod(r, TOKEN_TILES)
+            x_raw[r] = raw_pool.tile([P, ROUND_K], BF16, name="x_raw", tag="x_raw")
+            nc.sync.dma_start(
+                out=x_raw[r][:],
+                in_=x_rows[i * P : (i + 1) * P, chunk * ROUND_K : (chunk + 1) * ROUND_K],
+            )
+
+        def load_weights_piece(piece):
+            if piece < PIECES:
+                w1_words[piece] = weights.tile(
+                    [P, PIECE_PASSES, P1], U32, name="w1_words_%d" % piece, align_bytes=64
+                )
+                nc.sync.dma_start(
+                    out=w1_words[piece][:].bitcast(I32),
+                    in_=w1_words_dram[:, piece * PIECE_PASSES : (piece + 1) * PIECE_PASSES, :],
+                )
+            elif piece == PIECES:
+                nc.sync.dma_start(out=w2_words[:].bitcast(I32), in_=w2_words_dram)
+
+        def load_round(r):
+            load_x(r)
+            load_weights_piece(r + PIECES_AHEAD)
+
+        def sort_round(r):
+            x_sorted[r] = work.tile([P, ROUND_PASSES, PAIRS, P], F32, name="x_sorted", tag="x_sorted")
+            nc.vector.tensor_copy(
+                out=x_sorted[r][:],
+                in_=x_raw[r][:].bitcast(F32).rearrange("k (g p u) -> k g u p", g=ROUND_PASSES, u=PAIRS),
+            )
+            if r + X_BUFS < ROUNDS:
+                load_round(r + X_BUFS)
+
+        def transpose_round(r):
+            x_grouped[r] = work.tile(
+                [P, ROUND_PASSES, P, PACK], BF16, name="x_grouped", tag="x_grouped", align_bytes=64
+            )
+            grouped_words = (
+                x_grouped[r][:]
+                .rearrange("p g k t -> p (g k t)")
+                .bitcast(F32)
+                .rearrange("p (g k u) -> p g k u", g=ROUND_PASSES, u=PAIRS)
+            )
+            for b in range(ROUND_PASSES // BANK_PASSES):
+                xt = psum.tile([P, BANK_PASSES, PAIRS, P], F32, name="xt", tag="bank")
+                for g in range(BANK_PASSES):
+                    for u in range(PAIRS):
+                        nc.tensor.transpose(
+                            xt[:, g, u, :], x_sorted[r][:, b * BANK_PASSES + g, u, :], ident_f32[:]
+                        )
+                nc.scalar.copy(
+                    out=grouped_words[:, b * BANK_PASSES : (b + 1) * BANK_PASSES, :, :],
+                    in_=xt[:].rearrange("p g u k -> p g k u"),
+                )
+
+        def quantise_round(r):
+            x_codes[r] = work.tile([P, ROUND_PASSES, P], U32, name="x_codes", tag="x_codes", align_bytes=64)
+            x_scales[r] = work.tile([P, ROUND_PASSES, P], U8, name="x_scales", tag="x_scales", align_bytes=64)
+            nc.vector.quantize_mx(
+                out=x_codes[r][:].rearrange("p g k -> p (g k)").bitcast(FP8X4),
+                scales=x_scales[r][:].rearrange("p g k -> p (g k)"),
+                in_=x_grouped[r][:].rearrange("p g k t -> p (g k t)"),
+            )
+
+        def multiply_round(r):
+            chunk, i = divmod(r, TOKEN_TILES)
+            if chunk == 0:
+                h_acc[i] = psum.tile([P, P1], F32, name="h_acc_%d" % i, tag="bank")
+            for g in range(ROUND_PASSES):
+                g_all = chunk * ROUND_PASSES + g
+                piece, in_piece = divmod(g_all, PIECE_PASSES)
+                slot, plane = divmod(g_all, SHARED_PLANES)
+                nc.tensor.matmul_mx(
+                    out=h_acc[i][:],
+                    lhsT=x_codes[r][:, g, :].bitcast(FP8X4),
+                    lhsT_scale=x_scales[r][:, g, :],
+                    rhs=w1_words[piece][:, in_piece, :].bitcast(FP8X4),
+                    rhs_scale=w1_planes[plane * PLANE_STEP : P, slot, :],
+                    start=(g_all == 0),
+                    stop=(g_all == PASSES - 1),
+                )
+
+        def round_h(i):
+            h_bf16[i] = work.tile([P, PACK, P], BF16, name="h_bf16", tag="h_bf16")
+            nc.scalar.copy(out=h_bf16[i][:], in_=h_acc[i][:].rearrange("k (p t) -> k t p", t=PACK))
+
+        def transpose_h(i):
+            ht = psum.tile([P, PACK, P], BF16, name="ht", tag="bank")
+            for t in range(PACK):
+                nc.tensor.transpose(ht[:, t, :], h_bf16[i][:, t, :], ident_bf16[:])
+            h_grouped = work.tile([P, P, PACK], BF16, name="h_grouped", tag="h_grouped", align_bytes=64)
+            nc.scalar.copy(out=h_grouped[:], in_=ht[:].rearrange("p t k -> p k t"))
+            return h_grouped
+
+        def quantise_h(i, h_grouped):
+            h_codes[i] = work.tile([P, P], U32, name="h_codes", tag="h_codes", align_bytes=64)
+            h_scales[i] = work.tile([P, P], U8, name="h_scales", tag="h_scales", align_bytes=64)
+            nc.vector.quantize_mx(
+                out=h_codes[i][:].bitcast(FP8X4),
+                scales=h_scales[i][:],
+                in_=h_grouped[:].rearrange("p k t -> p (k t)"),
+            )
+
+        def multiply_h(i):
+            logits[i] = []
+            for half in range(HALVES):
+                cols = slice(half * BANK, (half + 1) * BANK)
+                bank = psum.tile([P, BANK], F32, name="logits", tag="bank")
+                nc.tensor.matmul_mx(
+                    out=bank[:],
+                    lhsT=h_codes[i][:].bitcast(FP8X4),
+                    lhsT_scale=h_scales[i][:],
+                    rhs=w2_words[:, cols].bitcast(FP8X4),
+                    rhs_scale=w2_plane[:, cols],
+                    start=True,
+                    stop=True,
+                )
+                logits[i].append(bank)
+
+        def row_max(i):
+            half_max = stats.tile([P, HALVES], F32, name="half_max", tag="half_max")
+            for half in range(HALVES):
+                nc.vector.reduce_max(
+                    out=half_max[:, half : half + 1], in_=logits[i][half][:], axis=mybir.AxisListType.X
+                )
+            neg_max[i] = stats.tile([P, 1], F32, name="neg_max", tag="neg_max")
+            nc.vector.tensor_scalar(
+                out=neg_max[i][:],
+                in0=half_max[:, 0:1],
+                scalar1=half_max[:, 1:2],
+                scalar2=-1.0,
+                op0=ALU.max,
+                op1=ALU.mult,
+            )
+
+        def exponentials(i):
+            probs[i] = probs_pool.tile([P, V2], F32, name="probs", tag="probs")
+            half_sum[i] = stats.tile([P, HALVES], F32, name="half_sum", tag="half_sum")
+            for half in range(HALVES):
+                nc.scalar.activation(
+                    out=probs[i][:, half * BANK : (half + 1) * BANK],
+                    in_=logits[i][half][:],
+                    func=EXP,
+                    bias=neg_max[i][:, 0:1],
+                    scale=1.0,
+                    accum_out=half_sum[i][:, half : half + 1],
+                )
+
+        def finish(i):
+            total = stats.tile([P, 1], F32, name="total", tag="total")
+            nc.vector.tensor_add(out=total[:], in0=half_sum[i][:, 0:1], in1=half_sum[i][:, 1:2])
+            inverse = stats.tile([P, 1], F32, name="inverse", tag="inverse")
+            nc.vector.reciprocal(out=inverse[:], in_=total[:])
+            nc.vector.tensor_scalar(
+                out=probs[i][:],
+                in0=probs[i][:],
+                scalar1=inverse[:, 0:1],
+                scalar2=prob_of_cluster[:, i : i + 1],
+                op0=ALU.mult,
+                op1=ALU.mult,
+            )
+            nc.sync.dma_start(out=out_rows[i * P : (i + 1) * P, :], in_=probs[i][:])
+
+        ident_f32 = const.tile([P, P], F32, name="ident_f32")
+        make_identity(nc, ident_f32[:])
+        ident_bf16 = const.tile([P, P], BF16, name="ident_bf16")
+        make_identity(nc, ident_bf16[:])
+
+        prob_rows = const.tile([P, P], BF16, name="prob_rows")
+        nc.vector.memset(prob_rows[:], 0.0)
+        nc.sync.dma_start(
+            out=prob_rows[0:TOKEN_TILES, :], in_=cluster_prob.rearrange("n (a k) o -> (n a) (k o)", k=P)
+        )
+        load_x(0)
+
+        w1_planes = const.tile([P, PLANE_SLOTS, P1], U8, name="w1_planes", align_bytes=64)
+        nc.vector.memset(w1_planes[:].bitcast(I32), 0)
+        w2_plane = const.tile([P, V2], U8, name="w2_plane", align_bytes=64)
+        nc.vector.memset(w2_plane[:].bitcast(I32), 0)
+        w2_words = const.tile([P, V2], U32, name="w2_words", align_bytes=64)
+        for c in range(P // QUADRANT):
+            for r in range(PLANE_STEP):
+                first = c * QUADRANT + r
+                nc.sync.dma_start(
+                    out=w1_planes[first : first + SHARED_PLANES * PLANE_STEP : PLANE_STEP, :, :].bitcast(I32),
+                    in_=w1_scales_dram[c * PLANE_STEP + r],
+                )
+        for r in range(PLANE_STEP):
+            nc.sync.dma_start(out=w2_plane[r:P:QUADRANT, :].bitcast(I32), in_=w2_scales_dram[r])
+
+        for piece in range(PIECES_AHEAD + 1):
+            load_weights_piece(piece)
+        for r in range(1, X_BUFS):
+            load_round(r)
+
+        warm = const.tile([P, 2], F32, name="warm")
+        nc.vector.memset(warm[:], 0.0)
+        nc.scalar.activation(out=warm[:, 1:2], in_=warm[:, 0:1], func=EXP)
+
+        prob_t = psum.tile([P, P], BF16, name="prob_t", tag="bank")
+        nc.tensor.transpose(prob_t[:], prob_rows[:], ident_bf16[:])
+        prob_of_cluster = const.tile([P, TOKEN_TILES], F32, name="prob_of_cluster")
+        nc.vector.tensor_copy(out=prob_of_cluster[:], in_=prob_t[:, 0:TOKEN_TILES])
+
+        sort_round(0)
+        for r in range(-1, ROUNDS + 3):
+            i = r - LAST_CHUNK
+            if r + 2 < ROUNDS:
+                sort_round(r + 2)
+            if r + 1 < ROUNDS:
+                transpose_round(r + 1)
+            h_grouped = None
+            if 0 <= i - 1 < TOKEN_TILES:
+                h_grouped = transpose_h(i - 1)
+            if 0 <= i - 2 < TOKEN_TILES:
+                exponentials(i - 2)
+            if r + 1 < ROUNDS:
+                quantise_round(r + 1)
+            if 0 <= i - 1 < TOKEN_TILES:
+                quantise_h(i - 1, h_grouped)
+            if 0 <= r < ROUNDS:
+                multiply_round(r)
+            if 0 <= i < TOKEN_TILES:
+                round_h(i)
+            if 0 <= i - 1 < TOKEN_TILES:
+                multiply_h(i - 1)
+            if 0 <= i - 3 < TOKEN_TILES:
+                finish(i - 3)
+            if 0 <= i - 1 < TOKEN_TILES:
+                row_max(i - 1)

@@ -31,14 +31,13 @@ CHUNKS = PASSES // ROUND_PASSES
 ROUNDS = CHUNKS * TOKEN_TILES
 LAST_CHUNK = ROUNDS - TOKEN_TILES
 BANK_PASSES = BANK // (PAIRS * P)
-PIECE_PASSES = 2
-PIECES = PASSES // PIECE_PASSES
-PIECES_AHEAD = 2
 X_BUFS = 8
 PLANE_STEP = 4
 SHARED_PLANES = 4
-PLANE_SLOTS = PASSES // SHARED_PLANES
+PIECE_PASSES = SHARED_PLANES
+PIECES = PASSES // PIECE_PASSES
 QUADRANT = 32
+QUADRANTS = P // QUADRANT
 HALVES = V2 // BANK
 
 FLOPS = 2 * TOKENS * D * P1 + 2 * TOKENS * P1 * V2
@@ -59,7 +58,7 @@ def tile_adaptiveinputsoftmax_pb_k_kernel(
     out_rows = out.flatten_outer_dims()
     w1_words_dram = tail_proj_1_words.rearrange("g p n t -> p g (n t)").bitcast(I32)
     w2_words_dram = tail_w_1_words.rearrange("o p n t -> (o p) (n t)").bitcast(I32)
-    w1_scales_dram = tail_proj_1_scales.bitcast(I32).rearrange("(s j) q n -> q j s n", j=SHARED_PLANES)
+    w1_scales_dram = tail_proj_1_scales.bitcast(I32)
     w2_scales_dram = tail_w_1_scales.bitcast(I32).rearrange("o (c r) n -> (o r) c n", r=PLANE_STEP)
 
     with ExitStack() as ctx:
@@ -97,19 +96,27 @@ def tile_adaptiveinputsoftmax_pb_k_kernel(
 
         def load_weights_piece(piece):
             if piece < PIECES:
+                passes = slice(piece * PIECE_PASSES, (piece + 1) * PIECE_PASSES)
+                for c in range(QUADRANTS):
+                    nc.sync.dma_start(
+                        out=w1_planes[
+                            c * QUADRANT : c * QUADRANT + SHARED_PLANES * PLANE_STEP, piece, :
+                        ].bitcast(I32),
+                        in_=w1_scales_dram[passes, c * PLANE_STEP : (c + 1) * PLANE_STEP, :],
+                    )
                 w1_words[piece] = weights.tile(
                     [P, PIECE_PASSES, P1], U32, name="w1_words_%d" % piece, align_bytes=64
                 )
-                nc.sync.dma_start(
-                    out=w1_words[piece][:].bitcast(I32),
-                    in_=w1_words_dram[:, piece * PIECE_PASSES : (piece + 1) * PIECE_PASSES, :],
-                )
+                nc.sync.dma_start(out=w1_words[piece][:].bitcast(I32), in_=w1_words_dram[:, passes, :])
             elif piece == PIECES:
+                for row in range(PLANE_STEP):
+                    nc.sync.dma_start(out=w2_plane[row:P:QUADRANT, :].bitcast(I32), in_=w2_scales_dram[row])
                 nc.sync.dma_start(out=w2_words[:].bitcast(I32), in_=w2_words_dram)
 
         def load_round(r):
             load_x(r)
-            load_weights_piece(r + PIECES_AHEAD)
+            if r % 2 == 1:
+                load_weights_piece((r + 1) // 2)
 
         def sort_round(r):
             x_sorted[r] = work.tile([P, ROUND_PASSES, PAIRS, P], F32, name="x_sorted", tag="x_sorted")
@@ -157,14 +164,13 @@ def tile_adaptiveinputsoftmax_pb_k_kernel(
                 h_acc[i] = psum.tile([P, P1], F32, name="h_acc_%d" % i, tag="bank")
             for g in range(ROUND_PASSES):
                 g_all = chunk * ROUND_PASSES + g
-                piece, in_piece = divmod(g_all, PIECE_PASSES)
-                slot, plane = divmod(g_all, SHARED_PLANES)
+                piece, plane = divmod(g_all, PIECE_PASSES)
                 nc.tensor.matmul_mx(
                     out=h_acc[i][:],
                     lhsT=x_codes[r][:, g, :].bitcast(FP8X4),
                     lhsT_scale=x_scales[r][:, g, :],
-                    rhs=w1_words[piece][:, in_piece, :].bitcast(FP8X4),
-                    rhs_scale=w1_planes[plane * PLANE_STEP : P, slot, :],
+                    rhs=w1_words[piece][:, plane, :].bitcast(FP8X4),
+                    rhs_scale=w1_planes[plane * PLANE_STEP : P, piece, :],
                     start=(g_all == 0),
                     stop=(g_all == PASSES - 1),
                 )
@@ -260,26 +266,18 @@ def tile_adaptiveinputsoftmax_pb_k_kernel(
         nc.sync.dma_start(
             out=prob_rows[0:TOKEN_TILES, :], in_=cluster_prob.rearrange("n (a k) o -> (n a) (k o)", k=P)
         )
-        load_x(0)
 
-        w1_planes = const.tile([P, PLANE_SLOTS, P1], U8, name="w1_planes", align_bytes=64)
+        w1_planes = const.tile([P, PIECES, P1], U8, name="w1_planes", align_bytes=64)
         nc.vector.memset(w1_planes[:].bitcast(I32), 0)
         w2_plane = const.tile([P, V2], U8, name="w2_plane", align_bytes=64)
         nc.vector.memset(w2_plane[:].bitcast(I32), 0)
         w2_words = const.tile([P, V2], U32, name="w2_words", align_bytes=64)
-        for c in range(P // QUADRANT):
-            for r in range(PLANE_STEP):
-                first = c * QUADRANT + r
-                nc.sync.dma_start(
-                    out=w1_planes[first : first + SHARED_PLANES * PLANE_STEP : PLANE_STEP, :, :].bitcast(I32),
-                    in_=w1_scales_dram[c * PLANE_STEP + r],
-                )
-        for r in range(PLANE_STEP):
-            nc.sync.dma_start(out=w2_plane[r:P:QUADRANT, :].bitcast(I32), in_=w2_scales_dram[r])
 
-        for piece in range(PIECES_AHEAD + 1):
-            load_weights_piece(piece)
-        for r in range(1, X_BUFS):
+        load_x(0)
+        load_x(1)
+        load_weights_piece(0)
+        load_weights_piece(1)
+        for r in range(2, X_BUFS):
             load_round(r)
 
         warm = const.tile([P, 2], F32, name="warm")

@@ -246,15 +246,17 @@ def tile_adaptiveinputsoftmax_pb_k_kernel(
             nc.vector.tensor_add(out=total[:], in0=half_sum[i][:, 0:1], in1=half_sum[i][:, 1:2])
             inverse = stats.tile([P, 1], F32, name="inverse", tag="inverse")
             nc.vector.reciprocal(out=inverse[:], in_=total[:])
-            nc.vector.tensor_scalar(
-                out=probs[i][:],
-                in0=probs[i][:],
-                scalar1=inverse[:, 0:1],
-                scalar2=prob_of_cluster[:, i : i + 1],
-                op0=ALU.mult,
-                op1=ALU.mult,
-            )
-            nc.sync.dma_start(out=out_rows[i * P : (i + 1) * P, :], in_=probs[i][:])
+            for half in range(HALVES):
+                cols = slice(half * BANK, (half + 1) * BANK)
+                nc.vector.tensor_scalar(
+                    out=probs[i][:, cols],
+                    in0=probs[i][:, cols],
+                    scalar1=inverse[:, 0:1],
+                    scalar2=prob_of_cluster[:, i : i + 1],
+                    op0=ALU.mult,
+                    op1=ALU.mult,
+                )
+                nc.sync.dma_start(out=out_rows[i * P : (i + 1) * P, cols], in_=probs[i][:, cols])
 
         ident_f32 = const.tile([P, P], F32, name="ident_f32")
         make_identity(nc, ident_f32[:])
@@ -296,15 +298,12 @@ def tile_adaptiveinputsoftmax_pb_k_kernel(
                 sort_round(r + 2)
             if r + 1 < ROUNDS:
                 transpose_round(r + 1)
-            h_grouped = None
             if 0 <= i - 1 < TOKEN_TILES:
-                h_grouped = transpose_h(i - 1)
+                quantise_h(i - 1, transpose_h(i - 1))
             if 0 <= i - 2 < TOKEN_TILES:
                 exponentials(i - 2)
             if r + 1 < ROUNDS:
                 quantise_round(r + 1)
-            if 0 <= i - 1 < TOKEN_TILES:
-                quantise_h(i - 1, h_grouped)
             if 0 <= r < ROUNDS:
                 multiply_round(r)
             if 0 <= i < TOKEN_TILES:

@@ -86,13 +86,24 @@ def tile_adaptiveinputsoftmax_pb_k_kernel(
         probs = {}
         half_sum = {}
 
+        def sort_parts(r):
+            return 4
+
+        def quant_parts(r):
+            return 4
+
+        def load_parts(r):
+            return 2 if r >= ROUNDS - 2 else 1
+
         def load_x(r):
             chunk, i = divmod(r, TOKEN_TILES)
             x_raw[r] = raw_pool.tile([P, ROUND_K], BF16, name="x_raw", tag="x_raw")
-            nc.sync.dma_start(
-                out=x_raw[r][:],
-                in_=x_rows[i * P : (i + 1) * P, chunk * ROUND_K : (chunk + 1) * ROUND_K],
-            )
+            width = ROUND_K // load_parts(r)
+            for first in range(0, ROUND_K, width):
+                start = chunk * ROUND_K + first
+                nc.sync.dma_start(
+                    out=x_raw[r][:, first : first + width], in_=x_rows[i * P : (i + 1) * P, start : start + width]
+                )
 
         def load_weights_piece(piece):
             if piece < PIECES:
@@ -115,16 +126,17 @@ def tile_adaptiveinputsoftmax_pb_k_kernel(
 
         def load_round(r):
             load_x(r)
-            if r % 2 == 1:
-                load_weights_piece((r + 1) // 2)
+            for piece in {3: [2], 5: [3], 7: [4], 9: [5], 11: [6], 13: [7], 15: [8]}.get(r, []):
+                load_weights_piece(piece)
 
-        def sort_round(r):
-            x_sorted[r] = work.tile([P, ROUND_PASSES, PAIRS, P], F32, name="x_sorted", tag="x_sorted")
-            nc.vector.tensor_copy(
-                out=x_sorted[r][:],
-                in_=x_raw[r][:].bitcast(F32).rearrange("k (g p u) -> k g u p", g=ROUND_PASSES, u=PAIRS),
-            )
-            if r + X_BUFS < ROUNDS:
+        def sort_part(r, which):
+            if which == 0:
+                x_sorted[r] = work.tile([P, ROUND_PASSES, PAIRS, P], F32, name="x_sorted", tag="x_sorted")
+            sort_from = x_raw[r][:].bitcast(F32).rearrange("k (g p u) -> k g u p", g=ROUND_PASSES, u=PAIRS)
+            count = ROUND_PASSES // sort_parts(r)
+            part = slice(which * count, (which + 1) * count)
+            nc.vector.tensor_copy(out=x_sorted[r][:, part, :, :], in_=sort_from[:, part, :, :])
+            if r + X_BUFS < ROUNDS and which == sort_parts(r) - 1:
                 load_round(r + X_BUFS)
 
         def transpose_round(r):
@@ -149,20 +161,23 @@ def tile_adaptiveinputsoftmax_pb_k_kernel(
                     in_=xt[:].rearrange("p g u k -> p g k u"),
                 )
 
-        def quantise_round(r):
-            x_codes[r] = work.tile([P, ROUND_PASSES, P], U32, name="x_codes", tag="x_codes", align_bytes=64)
-            x_scales[r] = work.tile([P, ROUND_PASSES, P], U8, name="x_scales", tag="x_scales", align_bytes=64)
+        def quantise_part(r, which):
+            if which == 0:
+                x_codes[r] = work.tile([P, ROUND_PASSES, P], U32, name="x_codes", tag="x_codes", align_bytes=64)
+                x_scales[r] = work.tile([P, ROUND_PASSES, P], U8, name="x_scales", tag="x_scales", align_bytes=64)
+            count = ROUND_PASSES // quant_parts(r)
+            part = slice(which * count, (which + 1) * count)
             nc.vector.quantize_mx(
-                out=x_codes[r][:].rearrange("p g k -> p (g k)").bitcast(FP8X4),
-                scales=x_scales[r][:].rearrange("p g k -> p (g k)"),
-                in_=x_grouped[r][:].rearrange("p g k t -> p (g k t)"),
+                out=x_codes[r][:, part, :].rearrange("p g k -> p (g k)").bitcast(FP8X4),
+                scales=x_scales[r][:, part, :].rearrange("p g k -> p (g k)"),
+                in_=x_grouped[r][:, part, :, :].rearrange("p g k t -> p (g k t)"),
             )
 
-        def multiply_round(r):
+        def multiply_round(r, begin=0, end=ROUND_PASSES):
             chunk, i = divmod(r, TOKEN_TILES)
             if chunk == 0:
                 h_acc[i] = psum.tile([P, P1], F32, name="h_acc_%d" % i, tag="bank")
-            for g in range(ROUND_PASSES):
+            for g in range(begin, end):
                 g_all = chunk * ROUND_PASSES + g
                 piece, plane = divmod(g_all, PIECE_PASSES)
                 nc.tensor.matmul_mx(
@@ -265,9 +280,12 @@ def tile_adaptiveinputsoftmax_pb_k_kernel(
 
         prob_rows = const.tile([P, P], BF16, name="prob_rows")
         nc.vector.memset(prob_rows[:], 0.0)
-        nc.sync.dma_start(
-            out=prob_rows[0:TOKEN_TILES, :], in_=cluster_prob.rearrange("n (a k) o -> (n a) (k o)", k=P)
-        )
+        prob_of_cluster = const.tile([P, TOKEN_TILES], F32, name="prob_of_cluster")
+
+        def spread_prob():
+            prob_t = psum.tile([P, P], BF16, name="prob_t", tag="bank")
+            nc.tensor.transpose(prob_t[:], prob_rows[:], ident_bf16[:])
+            nc.vector.tensor_copy(out=prob_of_cluster[:], in_=prob_t[:, 0:TOKEN_TILES])
 
         w1_planes = const.tile([P, PIECES, P1], U8, name="w1_planes", align_bytes=64)
         nc.vector.memset(w1_planes[:].bitcast(I32), 0)
@@ -278,36 +296,51 @@ def tile_adaptiveinputsoftmax_pb_k_kernel(
         load_x(0)
         load_x(1)
         load_weights_piece(0)
+        nc.sync.dma_start(
+            out=prob_rows[0:TOKEN_TILES, :], in_=cluster_prob.rearrange("n (a k) o -> (n a) (k o)", k=P)
+        )
+        load_x(2)
         load_weights_piece(1)
-        for r in range(2, X_BUFS):
+        for r in range(3, X_BUFS):
             load_round(r)
 
         warm = const.tile([P, 2], F32, name="warm")
         nc.vector.memset(warm[:], 0.0)
         nc.scalar.activation(out=warm[:, 1:2], in_=warm[:, 0:1], func=EXP)
 
-        prob_t = psum.tile([P, P], BF16, name="prob_t", tag="bank")
-        nc.tensor.transpose(prob_t[:], prob_rows[:], ident_bf16[:])
-        prob_of_cluster = const.tile([P, TOKEN_TILES], F32, name="prob_of_cluster")
-        nc.vector.tensor_copy(out=prob_of_cluster[:], in_=prob_t[:, 0:TOKEN_TILES])
-
-        sort_round(0)
+        for which in range(sort_parts(0)):
+            sort_part(0, which)
         for r in range(-1, ROUNDS + 3):
             i = r - LAST_CHUNK
-            if r + 2 < ROUNDS:
-                sort_round(r + 2)
+            sorts = [(r + 2, j) for j in range(sort_parts(r + 2))] if r + 2 < ROUNDS else []
+            quants = [(r + 1, j) for j in range(quant_parts(r + 1))] if r + 1 < ROUNDS else []
             if r + 1 < ROUNDS:
                 transpose_round(r + 1)
+            if r == 1:
+                spread_prob()
+            if r == ROUNDS - 1:
+                multiply_round(r, 0, ROUND_PASSES // 2)
             if 0 <= i - 1 < TOKEN_TILES:
-                quantise_h(i - 1, transpose_h(i - 1))
-            if 0 <= i - 2 < TOKEN_TILES:
+                h_ready = transpose_h(i - 1)
+            if r == ROUNDS - 1:
+                multiply_round(r, ROUND_PASSES // 2, ROUND_PASSES)
+            if 0 <= i - 2 < TOKEN_TILES and i != TOKEN_TILES - 1:
                 exponentials(i - 2)
-            if r + 1 < ROUNDS:
-                quantise_round(r + 1)
-            if 0 <= r < ROUNDS:
+            for letter in ("ssssqqqhq"):
+                if letter == "s" and sorts:
+                    sort_part(*sorts[0])
+                    sorts = sorts[1:]
+                if letter == "q" and quants:
+                    quantise_part(*quants[0])
+                    quants = quants[1:]
+                if letter == "h" and 0 <= i - 1 < TOKEN_TILES:
+                    quantise_h(i - 1, h_ready)
+            if 0 <= r < ROUNDS - 1:
                 multiply_round(r)
             if 0 <= i < TOKEN_TILES:
                 round_h(i)
+            if i == TOKEN_TILES - 1:
+                exponentials(i - 2)
             if 0 <= i - 1 < TOKEN_TILES:
                 multiply_h(i - 1)
             if 0 <= i - 3 < TOKEN_TILES:

@@ -324,9 +324,7 @@ def tile_adaptiveinputsoftmax_pb_k_kernel(
                 h_ready = transpose_h(i - 1)
             if r == ROUNDS - 1:
                 multiply_round(r, ROUND_PASSES // 2, ROUND_PASSES)
-            if 0 <= i - 2 < TOKEN_TILES and i != TOKEN_TILES - 1:
-                exponentials(i - 2)
-            for letter in ("ssssqqqhq"):
+            for letter in ("ssssqqqhq" if r < 12 else "ssqqhssqq"):
                 if letter == "s" and sorts:
                     sort_part(*sorts[0])
                     sorts = sorts[1:]
@@ -339,7 +337,7 @@ def tile_adaptiveinputsoftmax_pb_k_kernel(
                 multiply_round(r)
             if 0 <= i < TOKEN_TILES:
                 round_h(i)
-            if i == TOKEN_TILES - 1:
+            if 0 <= i - 2 < TOKEN_TILES:
                 exponentials(i - 2)
             if 0 <= i - 1 < TOKEN_TILES:
                 multiply_h(i - 1)

@@ -28,7 +28,13 @@ PASSES = D // K_PASS
 ROUND_PASSES = 8
 ROUND_K = ROUND_PASSES * K_PASS
 CHUNKS = PASSES // ROUND_PASSES
-ROUNDS = CHUNKS * TOKEN_TILES
+ROUND_PARTS = [
+    (0, 2, 0),
+    (2, 2, 0),
+    (0, 2, ROUND_PASSES // 2),
+    (2, 2, ROUND_PASSES // 2),
+] + [(i, 1, chunk * ROUND_PASSES) for chunk in range(1, CHUNKS) for i in range(TOKEN_TILES)]
+ROUNDS = len(ROUND_PARTS)
 LAST_CHUNK = ROUNDS - TOKEN_TILES
 BANK_PASSES = BANK // (PAIRS * P)
 X_BUFS = 8
@@ -56,6 +62,7 @@ def tile_adaptiveinputsoftmax_pb_k_kernel(
     nc = tc.nc
     x_rows = x.flatten_outer_dims()
     out_rows = out.flatten_outer_dims()
+    x_tiles = x_rows.rearrange("(i k) d -> k i d", k=P)
     w1_words_dram = tail_proj_1_words.rearrange("g p n t -> p g (n t)").bitcast(I32)
     w2_words_dram = tail_w_1_words.rearrange("o p n t -> (o p) (n t)").bitcast(I32)
     w1_scales_dram = tail_proj_1_scales.bitcast(I32)
@@ -96,14 +103,23 @@ def tile_adaptiveinputsoftmax_pb_k_kernel(
             return 2 if r >= ROUNDS - 2 else 1
 
         def load_x(r):
-            chunk, i = divmod(r, TOKEN_TILES)
+            first_tile, tiles, first_pass = ROUND_PARTS[r]
             x_raw[r] = raw_pool.tile([P, ROUND_K], BF16, name="x_raw", tag="x_raw")
-            width = ROUND_K // load_parts(r)
-            for first in range(0, ROUND_K, width):
-                start = chunk * ROUND_K + first
+            columns = ROUND_K // tiles
+            start = first_pass * K_PASS
+            if tiles > 1 and load_parts(r) == 1:
                 nc.sync.dma_start(
-                    out=x_raw[r][:, first : first + width], in_=x_rows[i * P : (i + 1) * P, start : start + width]
+                    out=x_raw[r][:].rearrange("k (i c) -> k i c", i=tiles),
+                    in_=x_tiles[:, first_tile : first_tile + tiles, start : start + columns],
                 )
+            else:
+                width = min(columns, ROUND_K // load_parts(r))
+                for i in range(tiles):
+                    for first in range(0, columns, width):
+                        nc.sync.dma_start(
+                            out=x_raw[r][:, i * columns + first : i * columns + first + width],
+                            in_=x_tiles[:, first_tile + i, start + first : start + first + width],
+                        )
 
         def load_weights_piece(piece):
             if piece < PIECES:
@@ -174,11 +190,13 @@ def tile_adaptiveinputsoftmax_pb_k_kernel(
             )
 
         def multiply_round(r, begin=0, end=ROUND_PASSES):
-            chunk, i = divmod(r, TOKEN_TILES)
-            if chunk == 0:
-                h_acc[i] = psum.tile([P, P1], F32, name="h_acc_%d" % i, tag="bank")
+            first_tile, tiles, first_pass = ROUND_PARTS[r]
             for g in range(begin, end):
-                g_all = chunk * ROUND_PASSES + g
+                turn, place = divmod(g, ROUND_PASSES // tiles)
+                i = first_tile + turn
+                g_all = first_pass + place
+                if g_all == 0:
+                    h_acc[i] = psum.tile([P, P1], F32, name="h_acc_%d" % i, tag="bank")
                 piece, plane = divmod(g_all, PIECE_PASSES)
                 nc.tensor.matmul_mx(
                     out=h_acc[i][:],

from contextlib import ExitStack

import concourse.mybir as mybir
from concourse.masks import make_identity

F32 = mybir.dt.float32
BF16 = mybir.dt.bfloat16
I32 = mybir.dt.int32
U32 = mybir.dt.uint32
U8 = mybir.dt.uint8
FP8X4 = mybir.dt.float8_e4m3fn_x4
EXP = mybir.ActivationFunctionType.Exp
ALU = mybir.AluOpType

P = 128
PACK = 4
K_PASS = P * PACK
PAIRS = PACK // 2
TOKENS = 512
D = 16384
P1 = 512
V2 = 1024
BANK = 512
PSUM_BANKS = 8

TOKEN_TILES = TOKENS // P
PASSES = D // K_PASS
ROUND_PASSES = 8
ROUND_K = ROUND_PASSES * K_PASS
CHUNKS = PASSES // ROUND_PASSES
ROUND_PARTS = [
    (0, 2, 0),
    (2, 2, 0),
    (0, 2, ROUND_PASSES // 2),
    (2, 2, ROUND_PASSES // 2),
] + [(i, 1, chunk * ROUND_PASSES) for chunk in range(1, CHUNKS) for i in range(TOKEN_TILES)]
ROUNDS = len(ROUND_PARTS)
LAST_CHUNK = ROUNDS - TOKEN_TILES
BANK_PASSES = BANK // (PAIRS * P)
X_BUFS = 8
PLANE_STEP = 4
SHARED_PLANES = 4
PIECE_PASSES = SHARED_PLANES
PIECES = PASSES // PIECE_PASSES
QUADRANT = 32
QUADRANTS = P // QUADRANT
HALVES = V2 // BANK

FLOPS = 2 * TOKENS * D * P1 + 2 * TOKENS * P1 * V2


def tile_adaptiveinputsoftmax_pb_k_kernel(
    tc,
    x,
    tail_proj_1_words,
    tail_proj_1_scales,
    tail_w_1_words,
    tail_w_1_scales,
    cluster_prob,
    out,
):
    nc = tc.nc
    x_rows = x.flatten_outer_dims()
    out_rows = out.flatten_outer_dims()
    x_tiles = x_rows.rearrange("(i k) d -> k i d", k=P)
    w1_words_dram = tail_proj_1_words.rearrange("g p n t -> p g (n t)").bitcast(I32)
    w2_words_dram = tail_w_1_words.rearrange("o p n t -> (o p) (n t)").bitcast(I32)
    w1_scales_dram = tail_proj_1_scales.bitcast(I32)
    w2_scales_dram = tail_w_1_scales.bitcast(I32).rearrange("o (c r) n -> (o r) c n", r=PLANE_STEP)

    with ExitStack() as ctx:
        ctx.enter_context(tc.manual_schedule())
        const = ctx.enter_context(tc.tile_pool(name="const", bufs=1))
        weights = ctx.enter_context(tc.tile_pool(name="weights", bufs=1))
        raw_pool = ctx.enter_context(tc.tile_pool(name="raw", bufs=X_BUFS))
        work = ctx.enter_context(tc.tile_pool(name="work", bufs=2))
        probs_pool = ctx.enter_context(tc.tile_pool(name="probs", bufs=3))
        stats = ctx.enter_context(tc.tile_pool(name="stats", bufs=4))
        psum = ctx.enter_context(tc.psum_pool(name="psum", bufs=PSUM_BANKS))

        x_raw = {}
        x_sorted = {}
        x_grouped = {}
        x_codes = {}
        x_scales = {}
        w1_words = {}
        h_acc = {}
        h_bf16 = {}
        h_codes = {}
        h_scales = {}
        logits = {}
        neg_max = {}
        probs = {}
        half_sum = {}

        def sort_parts(r):
            return 4

        def quant_parts(r):
            return 4

        def load_parts(r):
            return 2 if r >= ROUNDS - 2 else 1

        def load_x(r):
            first_tile, tiles, first_pass = ROUND_PARTS[r]
            x_raw[r] = raw_pool.tile([P, ROUND_K], BF16, name="x_raw", tag="x_raw")
            columns = ROUND_K // tiles
            start = first_pass * K_PASS
            if tiles > 1 and load_parts(r) == 1:
                nc.sync.dma_start(
                    out=x_raw[r][:].rearrange("k (i c) -> k i c", i=tiles),
                    in_=x_tiles[:, first_tile : first_tile + tiles, start : start + columns],
                )
            else:
                width = min(columns, ROUND_K // load_parts(r))
                for i in range(tiles):
                    for first in range(0, columns, width):
                        nc.sync.dma_start(
                            out=x_raw[r][:, i * columns + first : i * columns + first + width],
                            in_=x_tiles[:, first_tile + i, start + first : start + first + width],
                        )

        def load_weights_piece(piece):
            if piece < PIECES:
                passes = slice(piece * PIECE_PASSES, (piece + 1) * PIECE_PASSES)
                for c in range(QUADRANTS):
                    nc.sync.dma_start(
                        out=w1_planes[
                            c * QUADRANT : c * QUADRANT + SHARED_PLANES * PLANE_STEP, piece, :
                        ].bitcast(I32),
                        in_=w1_scales_dram[passes, c * PLANE_STEP : (c + 1) * PLANE_STEP, :],
                    )
                w1_words[piece] = weights.tile(
                    [P, PIECE_PASSES, P1], U32, name="w1_words_%d" % piece, align_bytes=64
                )
                nc.sync.dma_start(out=w1_words[piece][:].bitcast(I32), in_=w1_words_dram[:, passes, :])
            elif piece == PIECES:
                for row in range(PLANE_STEP):
                    nc.sync.dma_start(out=w2_plane[row:P:QUADRANT, :].bitcast(I32), in_=w2_scales_dram[row])
                nc.sync.dma_start(out=w2_words[:].bitcast(I32), in_=w2_words_dram)

        def load_round(r):
            load_x(r)
            for piece in {3: [2], 5: [3], 7: [4], 9: [5], 11: [6], 13: [7], 15: [8]}.get(r, []):
                load_weights_piece(piece)

        def sort_part(r, which):
            if which == 0:
                x_sorted[r] = work.tile([P, ROUND_PASSES, PAIRS, P], F32, name="x_sorted", tag="x_sorted")
            sort_from = x_raw[r][:].bitcast(F32).rearrange("k (g p u) -> k g u p", g=ROUND_PASSES, u=PAIRS)
            count = ROUND_PASSES // sort_parts(r)
            part = slice(which * count, (which + 1) * count)
            nc.vector.tensor_copy(out=x_sorted[r][:, part, :, :], in_=sort_from[:, part, :, :])
            if r + X_BUFS < ROUNDS and which == sort_parts(r) - 1:
                load_round(r + X_BUFS)

        def transpose_round(r):
            x_grouped[r] = work.tile(
                [P, ROUND_PASSES, P, PACK], BF16, name="x_grouped", tag="x_grouped", align_bytes=64
            )
            grouped_words = (
                x_grouped[r][:]
                .rearrange("p g k t -> p (g k t)")
                .bitcast(F32)
                .rearrange("p (g k u) -> p g k u", g=ROUND_PASSES, u=PAIRS)
            )
            for b in range(ROUND_PASSES // BANK_PASSES):
                xt = psum.tile([P, BANK_PASSES, PAIRS, P], F32, name="xt", tag="bank")
                for g in range(BANK_PASSES):
                    for u in range(PAIRS):
                        nc.tensor.transpose(
                            xt[:, g, u, :], x_sorted[r][:, b * BANK_PASSES + g, u, :], ident_f32[:]
                        )
                nc.scalar.copy(
                    out=grouped_words[:, b * BANK_PASSES : (b + 1) * BANK_PASSES, :, :],
                    in_=xt[:].rearrange("p g u k -> p g k u"),
                )

        def quantise_part(r, which):
            if which == 0:
                x_codes[r] = work.tile([P, ROUND_PASSES, P], U32, name="x_codes", tag="x_codes", align_bytes=64)
                x_scales[r] = work.tile([P, ROUND_PASSES, P], U8, name="x_scales", tag="x_scales", align_bytes=64)
            count = ROUND_PASSES // quant_parts(r)
            part = slice(which * count, (which + 1) * count)
            nc.vector.quantize_mx(
                out=x_codes[r][:, part, :].rearrange("p g k -> p (g k)").bitcast(FP8X4),
                scales=x_scales[r][:, part, :].rearrange("p g k -> p (g k)"),
                in_=x_grouped[r][:, part, :, :].rearrange("p g k t -> p (g k t)"),
            )

        def multiply_round(r, begin=0, end=ROUND_PASSES):
            first_tile, tiles, first_pass = ROUND_PARTS[r]
            for g in range(begin, end):
                turn, place = divmod(g, ROUND_PASSES // tiles)
                i = first_tile + turn
                g_all = first_pass + place
                if g_all == 0:
                    h_acc[i] = psum.tile([P, P1], F32, name="h_acc_%d" % i, tag="bank")
                piece, plane = divmod(g_all, PIECE_PASSES)
                nc.tensor.matmul_mx(
                    out=h_acc[i][:],
                    lhsT=x_codes[r][:, g, :].bitcast(FP8X4),
                    lhsT_scale=x_scales[r][:, g, :],
                    rhs=w1_words[piece][:, plane, :].bitcast(FP8X4),
                    rhs_scale=w1_planes[plane * PLANE_STEP : P, piece, :],
                    start=(g_all == 0),
                    stop=(g_all == PASSES - 1),
                )

        def round_h(i):
            h_bf16[i] = work.tile([P, PACK, P], BF16, name="h_bf16", tag="h_bf16")
            nc.scalar.copy(out=h_bf16[i][:], in_=h_acc[i][:].rearrange("k (p t) -> k t p", t=PACK))

        def transpose_h(i):
            ht = psum.tile([P, PACK, P], BF16, name="ht", tag="bank")
            for t in range(PACK):
                nc.tensor.transpose(ht[:, t, :], h_bf16[i][:, t, :], ident_bf16[:])
            h_grouped = work.tile([P, P, PACK], BF16, name="h_grouped", tag="h_grouped", align_bytes=64)
            nc.scalar.copy(out=h_grouped[:], in_=ht[:].rearrange("p t k -> p k t"))
            return h_grouped

        def quantise_h(i, h_grouped):
            h_codes[i] = work.tile([P, P], U32, name="h_codes", tag="h_codes", align_bytes=64)
            h_scales[i] = work.tile([P, P], U8, name="h_scales", tag="h_scales", align_bytes=64)
            nc.vector.quantize_mx(
                out=h_codes[i][:].bitcast(FP8X4),
                scales=h_scales[i][:],
                in_=h_grouped[:].rearrange("p k t -> p (k t)"),
            )

        def multiply_h(i):
            logits[i] = []
            for half in range(HALVES):
                cols = slice(half * BANK, (half + 1) * BANK)
                bank = psum.tile([P, BANK], F32, name="logits", tag="bank")
                nc.tensor.matmul_mx(
                    out=bank[:],
                    lhsT=h_codes[i][:].bitcast(FP8X4),
                    lhsT_scale=h_scales[i][:],
                    rhs=w2_words[:, cols].bitcast(FP8X4),
                    rhs_scale=w2_plane[:, cols],
                    start=True,
                    stop=True,
                )
                logits[i].append(bank)

        def row_max(i):
            half_max = stats.tile([P, HALVES], F32, name="half_max", tag="half_max")
            for half in range(HALVES):
                nc.vector.reduce_max(
                    out=half_max[:, half : half + 1], in_=logits[i][half][:], axis=mybir.AxisListType.X
                )
            neg_max[i] = stats.tile([P, 1], F32, name="neg_max", tag="neg_max")
            nc.vector.tensor_scalar(
                out=neg_max[i][:],
                in0=half_max[:, 0:1],
                scalar1=half_max[:, 1:2],
                scalar2=-1.0,
                op0=ALU.max,
                op1=ALU.mult,
            )

        def exponentials(i):
            probs[i] = probs_pool.tile([P, V2], F32, name="probs", tag="probs")
            half_sum[i] = stats.tile([P, HALVES], F32, name="half_sum", tag="half_sum")
            for half in range(HALVES):
                nc.scalar.activation(
                    out=probs[i][:, half * BANK : (half + 1) * BANK],
                    in_=logits[i][half][:],
                    func=EXP,
                    bias=neg_max[i][:, 0:1],
                    scale=1.0,
                    accum_out=half_sum[i][:, half : half + 1],
                )

        def finish(i):
            total = stats.tile([P, 1], F32, name="total", tag="total")
            nc.vector.tensor_add(out=total[:], in0=half_sum[i][:, 0:1], in1=half_sum[i][:, 1:2])
            inverse = stats.tile([P, 1], F32, name="inverse", tag="inverse")
            nc.vector.reciprocal(out=inverse[:], in_=total[:])
            for half in range(HALVES):
                cols = slice(half * BANK, (half + 1) * BANK)
                nc.vector.tensor_scalar(
                    out=probs[i][:, cols],
                    in0=probs[i][:, cols],
                    scalar1=inverse[:, 0:1],
                    scalar2=prob_of_cluster[:, i : i + 1],
                    op0=ALU.mult,
                    op1=ALU.mult,
                )
                nc.sync.dma_start(out=out_rows[i * P : (i + 1) * P, cols], in_=probs[i][:, cols])

        ident_f32 = const.tile([P, P], F32, name="ident_f32")
        make_identity(nc, ident_f32[:])
        ident_bf16 = const.tile([P, P], BF16, name="ident_bf16")
        make_identity(nc, ident_bf16[:])

        prob_rows = const.tile([P, P], BF16, name="prob_rows")
        nc.vector.memset(prob_rows[:], 0.0)
        prob_of_cluster = const.tile([P, TOKEN_TILES], F32, name="prob_of_cluster")

        def spread_prob():
            prob_t = psum.tile([P, P], BF16, name="prob_t", tag="bank")
            nc.tensor.transpose(prob_t[:], prob_rows[:], ident_bf16[:])
            nc.vector.tensor_copy(out=prob_of_cluster[:], in_=prob_t[:, 0:TOKEN_TILES])

        w1_planes = const.tile([P, PIECES, P1], U8, name="w1_planes", align_bytes=64)
        nc.vector.memset(w1_planes[:].bitcast(I32), 0)
        w2_plane = const.tile([P, V2], U8, name="w2_plane", align_bytes=64)
        nc.vector.memset(w2_plane[:].bitcast(I32), 0)
        w2_words = const.tile([P, V2], U32, name="w2_words", align_bytes=64)

        load_x(0)
        load_x(1)
        load_weights_piece(0)
        nc.sync.dma_start(
            out=prob_rows[0:TOKEN_TILES, :], in_=cluster_prob.rearrange("n (a k) o -> (n a) (k o)", k=P)
        )
        load_x(2)
        load_weights_piece(1)
        for r in range(3, X_BUFS):
            load_round(r)

        warm = const.tile([P, 2], F32, name="warm")
        nc.vector.memset(warm[:], 0.0)
        nc.scalar.activation(out=warm[:, 1:2], in_=warm[:, 0:1], func=EXP)

        for which in range(sort_parts(0)):
            sort_part(0, which)
        for r in range(-1, ROUNDS + 3):
            i = r - LAST_CHUNK
            sorts = [(r + 2, j) for j in range(sort_parts(r + 2))] if r + 2 < ROUNDS else []
            quants = [(r + 1, j) for j in range(quant_parts(r + 1))] if r + 1 < ROUNDS else []
            if r + 1 < ROUNDS:
                transpose_round(r + 1)
            if r == 1:
                spread_prob()
            if r == ROUNDS - 1:
                multiply_round(r, 0, ROUND_PASSES // 2)
            if 0 <= i - 1 < TOKEN_TILES:
                h_ready = transpose_h(i - 1)
            if r == ROUNDS - 1:
                multiply_round(r, ROUND_PASSES // 2, ROUND_PASSES)
            for letter in ("ssssqqqhq" if r < 12 else "ssqqhssqq"):
                if letter == "s" and sorts:
                    sort_part(*sorts[0])
                    sorts = sorts[1:]
                if letter == "q" and quants:
                    quantise_part(*quants[0])
                    quants = quants[1:]
                if letter == "h" and 0 <= i - 1 < TOKEN_TILES:
                    quantise_h(i - 1, h_ready)
            if 0 <= r < ROUNDS - 1:
                multiply_round(r)
            if 0 <= i < TOKEN_TILES:
                round_h(i)
            if 0 <= i - 2 < TOKEN_TILES:
                exponentials(i - 2)
            if 0 <= i - 1 < TOKEN_TILES:
                multiply_h(i - 1)
            if 0 <= i - 3 < TOKEN_TILES:
                finish(i - 3)
            if 0 <= i - 1 < TOKEN_TILES:
                row_max(i - 1)
